import numpy as np
import ml_dtypes


def mxq(x, axis, fmt="e4m3"):
    dtype, down = {"e4m3": (ml_dtypes.float8_e4m3fn, 7), "e5m2": (ml_dtypes.float8_e5m2, 14)}[fmt]
    v = np.moveaxis(np.asarray(x, np.float32).astype(ml_dtypes.bfloat16).astype(np.float64), axis, -1)
    blocks = v.reshape(v.shape[:-1] + (-1, 32))
    amax = np.abs(blocks).max(-1, keepdims=True)
    byte = np.maximum(np.where(amax > 0, np.frexp(amax)[1] - 1 + 127, 0) - down, 1)
    scale = np.exp2(byte - 127.0)
    codes = (blocks / scale).astype(np.float32).astype(dtype).astype(np.float64)
    return np.moveaxis((codes * scale).reshape(v.shape), -1, axis)


WIDE = False


def mx_kscale(k):
    if not WIDE:
        return np.ones(k)
    levels = np.array([10, -10, 5, -5, 0])
    a = np.random.permutation(np.resize(levels, k // 512 * 4)).reshape(k // 512, 4)
    idx = np.arange(k)
    return np.exp2(a[idx // 512, idx % 128 // 32])


BF16 = ml_dtypes.bfloat16


def bf(x):
    return np.asarray(x, np.float32).astype(BF16)


def f64(x):
    return np.asarray(x).astype(np.float64)


E2M1 = np.array([0.0, 0.5, 1.0, 1.5, 2.0, 3.0, 4.0, 6.0, -0.0, -0.5, -1.0, -1.5, -2.0, -3.0, -4.0, -6.0])


def pack_weight(w, fmt):
    k, n = w.shape
    w = f64(bf(w)).reshape(k // 32, 32, n)
    amax = np.abs(w).max(1)
    if fmt == "e4m3":
        byte = np.frexp(amax)[1] - 1 + 127 - 7
    else:
        mant, ex = np.frexp(amax / 6.0)
        byte = np.where(mant > 0.5, ex, ex - 1) + 127
    byte = np.clip(np.where(amax > 0, byte, 1), 1, 254)
    scaled = (w * np.exp2(127.0 - byte)[:, None, :]).reshape(k, n).astype(np.float32)
    by_word = np.ascontiguousarray(scaled.reshape(k // 512, 128, 4, n).transpose(0, 1, 3, 2))
    if fmt == "e4m3":
        words = by_word.astype(ml_dtypes.float8_e4m3fn).view(np.uint8)
    else:
        c = by_word.astype(ml_dtypes.float4_e2m1fn).view(np.uint8) & 0xF
        words = c[..., 0::2] | (c[..., 1::2] << 4)
    return np.ascontiguousarray(words), np.ascontiguousarray(byte.astype(np.uint8).reshape(k // 512, 16, n))


def unpack_weight(words, scales, fmt):
    g, p, n, _ = words.shape
    if fmt == "e4m3":
        vals = np.ascontiguousarray(words).view(ml_dtypes.float8_e4m3fn).astype(np.float64)
    else:
        nib = np.empty((g, p, n, 4), np.uint8)
        nib[..., 0::2] = words & 0xF
        nib[..., 1::2] = words >> 4
        vals = E2M1[nib]
    vals = vals * np.repeat(np.exp2(scales.astype(np.float64) - 127.0), 8, axis=1)[..., None]
    return vals.transpose(0, 1, 3, 2).reshape(g * 512, n)


IN, H, C, B = 1024, 1024, 2, 512
QH = H % 512 == 0


def sigmoid(v):
    return 1.0 / (1.0 + np.exp(-v))


def setup_inputs():
    s = mx_kscale(IN)
    t = mx_kscale(H) if QH else np.ones(H)
    input_word = bf(np.random.standard_normal((B, IN)) * s)
    hidden_states = bf(np.random.standard_normal((B, H)) * t)
    wx = np.random.uniform(-1.0, 1.0, (C, 2 * H, IN)) / np.sqrt(IN) / s
    cat = np.ascontiguousarray(wx.swapaxes(1, 2)).reshape(-1, 2 * H)
    words, scales = pack_weight(cat, "e4m3")
    bx = bf(np.random.standard_normal((C, 2 * H)) * 0.3)
    Wh = bf(np.random.uniform(-1.0, 1.0, (C, 2 * H, H)) / np.sqrt(H) / t)
    return {"input_word": input_word,
            "hidden_states": hidden_states,
            "Wx_words": words,
            "Wx_scales": scales,
            "bx": bx,
            "Wh": Wh}


def reference(input_word, hidden_states, Wx_words, Wx_scales, bx, Wh):
    px = mxq(f64(input_word), 1, "e4m3") @ unpack_weight(Wx_words, Wx_scales, "e4m3").reshape(C, IN, 2 * H)
    if QH:
        ph = mxq(f64(hidden_states), 1, "e4m3") @ mxq(f64(Wh), 2, "e4m3").transpose(0, 2, 1)
    else:
        ph = f64(hidden_states) @ f64(Wh).transpose(0, 2, 1)
    net = px.transpose(1, 0, 2) + ph.transpose(1, 0, 2) + f64(bx)[None, :, :]
    input_gate, cell_states = net[..., :H], net[..., H:]
    cell_input = np.tanh(cell_states)
    input_gate = sigmoid(input_gate)
    return (cell_input, input_gate)

@@ -1,0 +1,234 @@
+from contextlib import ExitStack
+
+import concourse.mybir as mybir
+from concourse.masks import make_identity
+
+F32 = mybir.dt.float32
+BF16 = mybir.dt.bfloat16
+I32 = mybir.dt.int32
+U32 = mybir.dt.uint32
+U8 = mybir.dt.uint8
+FP8X4 = mybir.dt.float8_e4m3fn_x4
+ACT = mybir.ActivationFunctionType
+
+P = 128
+PACK = 4
+PAIR = 2
+K_PASS = P * PACK
+BATCH = 512
+K = 1024
+HID = 1024
+CELLS = 2
+PASSES = K // K_PASS
+PASS_WORDS = K_PASS // PAIR
+B_TILES = BATCH // P
+CHUNK = 512
+SLABS = HID // CHUNK
+ROWS = CHUNK // P
+RESULT_BUFS = 20
+
+FLOPS = 2 * BATCH * (CELLS * 2 * HID) * (2 * K)
+
+
+def tile_compute_gate_e_kernel(tc, input_word, hidden_states, Wx_words, Wx_scales, bx, Wh, out_0, out_1):
+    nc = tc.nc
+
+    chunks = []
+    for func, out, first_n in ((ACT.Sigmoid, out_1, 0), (ACT.Tanh, out_0, HID)):
+        for cell in range(CELLS):
+            for slab in range(SLABS):
+                chunks.append((func, out, cell, slab * CHUNK, first_n + slab * CHUNK))
+    n_chunks = len(chunks)
+
+    with ExitStack() as ctx:
+        keep = ctx.enter_context(tc.tile_pool(name="keep", bufs=1))
+        act_stage = ctx.enter_context(tc.tile_pool(name="act_stage", bufs=3))
+        wh_stage = ctx.enter_context(tc.tile_pool(name="wh_stage", bufs=2))
+        results = ctx.enter_context(tc.tile_pool(name="results", bufs=RESULT_BUFS))
+        flip_banks = ctx.enter_context(tc.psum_pool(name="flip_banks", bufs=4))
+        sum_banks = ctx.enter_context(tc.psum_pool(name="sum_banks", bufs=B_TILES))
+        ctx.enter_context(tc.manual_schedule())
+
+        wx_planes = keep.tile([P, 2 * HID], U8, name="wx_planes", align_bytes=64)
+        nc.vector.memset(wx_planes[:].bitcast(I32), 0)
+        bias_rows = keep.tile([P, CHUNK], BF16, name="bias_rows")
+        nc.vector.memset(bias_rows[:], 0.0)
+        warm = keep.tile([P, 1], F32, name="warm")
+        nc.vector.memset(warm[:], 0.0)
+        nc.scalar.activation(out=warm[:], in_=warm[:], func=ACT.Sigmoid)
+        ident_f32 = keep.tile([P, P], F32, name="ident_f32")
+        make_identity(nc, ident_f32[:])
+        ident_bf16 = keep.tile([P, P], BF16, name="ident_bf16")
+        make_identity(nc, ident_bf16[:])
+
+        def load_activations(rows, name):
+            halves = []
+            for half in range(B_TILES // 2):
+                raw = keep.tile([P, 2, K], BF16, name="%s_raw%d" % (name, half))
+                nc.sync.dma_start(
+                    out=raw[:],
+                    in_=rows[2 * P * half : 2 * P * (half + 1), :].rearrange("(t p) k -> p t k", p=P),
+                )
+                halves.append(raw)
+            return halves
+
+        def load_wx(j):
+            cell, n0 = chunks[j][2], chunks[j][4]
+            words = keep.tile([P, PASSES, CHUNK], U32, name="wx_words%d" % j, align_bytes=64)
+            nc.sync.dma_start(
+                out=words[:].bitcast(I32),
+                in_=Wx_words[PASSES * cell : PASSES * (cell + 1), :, n0 : n0 + CHUNK, :]
+                .rearrange("g p n t -> p g (n t)")
+                .bitcast(I32),
+            )
+            return words
+
+        def load_wh(j):
+            cell, n0 = chunks[j][2], chunks[j][4]
+            raw = keep.tile([P, ROWS, K], BF16, name="wh_raw%d" % j)
+            rows = Wh[cell, n0 : n0 + CHUNK, :].rearrange("(q r) k -> q r k", r=ROWS)
+            for first in range(0, ROWS, PAIR):
+                nc.sync.dma_start(out=raw[:, first : first + PAIR, :], in_=rows[:, first : first + PAIR, :])
+            return raw
+
+        x_raw = load_activations(input_word, "x")
+        for quadrant in range(4):
+            nc.sync.dma_start(
+                out=wx_planes[32 * quadrant : 32 * quadrant + 16, :].bitcast(I32),
+                in_=Wx_scales[:, 4 * quadrant : 4 * quadrant + 4, :].bitcast(I32),
+            )
+        nc.sync.dma_start(out=bias_rows[0 : CELLS * 2 * SLABS, :], in_=bx.rearrange("c (s n) -> (c s) n", n=CHUNK))
+        wx_words = [load_wx(0)]
+        h_raw = load_activations(hidden_states, "h")
+        wh_raw = [load_wh(0)]
+        for j in range(1, n_chunks):
+            wh_raw.append(load_wh(j))
+            wx_words.append(load_wx(j))
+
+        def quantise_activations(raw_halves, word_columns, name):
+            codes = keep.tile([P, B_TILES, PASSES * P], U32, name="%s_codes" % name, align_bytes=64)
+            planes = keep.tile([P, B_TILES, PASSES * P], U8, name="%s_planes" % name, align_bytes=64)
+            for bt in range(B_TILES):
+                words = raw_halves[bt // 2][:, bt % 2, :].bitcast(F32)
+                flipped = flip_banks.tile([P, PASSES, PAIR, P], F32, name="flipped", tag="bank")
+                for g in range(PASSES):
+                    for u in range(PAIR):
+                        nc.tensor.transpose(flipped[:, g, u, :], words[:, word_columns(g, u)], ident_f32[:])
+                grouped = act_stage.tile([P, PASSES, P, PACK], BF16, name="grouped", align_bytes=64)
+                copy = nc.scalar.copy if bt % 2 == 0 else nc.vector.tensor_copy
+                copy(out=grouped[:].bitcast(F32), in_=flipped[:].rearrange("p g u b -> p g b u"))
+                nc.vector.quantize_mx(
+                    out=codes[:, bt, :].bitcast(FP8X4),
+                    scales=planes[:, bt, :],
+                    in_=grouped[:].rearrange("p g b t -> p (g b t)"),
+                )
+            return codes, planes
+
+        bias_all = keep.tile([P, CELLS * 2 * SLABS, CHUNK], BF16, name="bias_all")
+
+        def spread_bias(first_row):
+            spread = flip_banks.tile([P, PAIR, CHUNK], BF16, name="spread", tag="bank")
+            for i in range(PAIR):
+                row = first_row + i
+                nc.tensor.matmul(
+                    spread[:, i, :],
+                    lhsT=ident_bf16[:, row : row + 1].to_broadcast([P, P]),
+                    rhs=bias_rows[:],
+                    start=True,
+                    stop=True,
+                )
+            nc.vector.tensor_copy(out=bias_all[:, first_row : first_row + PAIR, :], in_=spread[:])
+
+        def transpose_wh(j):
+            words = wh_raw[j][:].bitcast(F32)
+            grouped = wh_stage.tile([P, PASSES, CHUNK, PACK], BF16, name="wh_grouped", align_bytes=64)
+            for first in range(0, ROWS, PAIR):
+                for g in range(PASSES):
+                    flipped = flip_banks.tile([P, PAIR, PAIR, P], F32, name="flipped", tag="bank")
+                    for r in range(PAIR):
+                        for u in range(PAIR):
+                            start_word = PASS_WORDS * g + P * u
+                            nc.tensor.transpose(
+                                flipped[:, r, u, :], words[:, first + r, start_word : start_word + P], ident_f32[:]
+                            )
+                    nc.scalar.copy(
+                        out=grouped[:, g].bitcast(F32).rearrange("p (q r) u -> p q r u", r=ROWS)[
+                            :, :, first : first + PAIR, :
+                        ],
+                        in_=flipped[:].rearrange("p r u q -> p q r u"),
+                    )
+            return grouped
+
+        def quantise_wh(grouped):
+            codes = wh_stage.tile([P, PASSES, CHUNK], U32, name="wh_codes", align_bytes=64)
+            planes = wh_stage.tile([P, PASSES, CHUNK], U8, name="wh_planes", align_bytes=64)
+            for g in range(PASSES):
+                nc.vector.quantize_mx(
+                    out=codes[:, g, :].bitcast(FP8X4),
+                    scales=planes[:, g, :],
+                    in_=grouped[:, g].rearrange("p n t -> p (n t)"),
+                )
+            return codes, planes
+
+        def open_sums(j):
+            cell, n0 = chunks[j][2], chunks[j][4]
+            sums = []
+            for bt in range(B_TILES):
+                bank = sum_banks.tile([P, CHUNK], F32, name="sums")
+                for g in range(PASSES):
+                    nc.tensor.matmul_mx(
+                        out=bank[:],
+                        lhsT=x_codes[:, bt, P * g : P * (g + 1)].bitcast(FP8X4),
+                        lhsT_scale=x_planes[:, bt, P * g : P * (g + 1)],
+                        rhs=wx_words[j][:, g, :].bitcast(FP8X4),
+                        rhs_scale=wx_planes[4 * (PASSES * cell + g) : P, n0 : n0 + CHUNK],
+                        start=(g == 0),
+                        stop=False,
+                    )
+                sums.append(bank)
+            return sums
+
+        def close_sums(j, sums, codes, planes):
+            func, out, cell, out_col, n0 = chunks[j]
+            for bt in range(B_TILES):
+                for g in range(PASSES):
+                    nc.tensor.matmul_mx(
+                        out=sums[bt][:],
+                        lhsT=h_codes[:, bt, P * g : P * (g + 1)].bitcast(FP8X4),
+                        lhsT_scale=h_planes[:, bt, P * g : P * (g + 1)],
+                        rhs=codes[:, g, :].bitcast(FP8X4),
+                        rhs_scale=planes[:, g, :],
+                        start=False,
+                        stop=(g == PASSES - 1),
+                    )
+            for bt in range(B_TILES):
+                result = results.tile([P, CHUNK], F32, name="result")
+                nc.vector.tensor_tensor(
+                    out=result[:],
+                    in0=sums[bt][:],
+                    in1=bias_all[:, 2 * SLABS * cell + n0 // CHUNK, :],
+                    op=mybir.AluOpType.add,
+                )
+                nc.scalar.activation(out=result[:], in_=result[:], func=func)
+                nc.sync.dma_start(out=out[P * bt : P * (bt + 1), cell, out_col : out_col + CHUNK], in_=result[:])
+
+        x_codes, x_planes = quantise_activations(
+            x_raw, lambda g, u: slice(PASS_WORDS * g + u, PASS_WORDS * (g + 1), PAIR), "x"
+        )
+        for cell in range(CELLS):
+            spread_bias(2 * SLABS * cell)
+        sums = open_sums(0)
+        h_codes, h_planes = quantise_activations(
+            h_raw, lambda g, u: slice(PASS_WORDS * g + P * u, PASS_WORDS * g + P * (u + 1)), "h"
+        )
+        codes, planes = quantise_wh(transpose_wh(0))
+        for cell in range(CELLS):
+            spread_bias(2 * SLABS * cell + SLABS)
+        for j in range(n_chunks):
+            last = j == n_chunks - 1
+            if not last:
+                next_grouped = transpose_wh(j + 1)
+            close_sums(j, sums, codes, planes)
+            if not last:
+                codes, planes = quantise_wh(next_grouped)
+                sums = open_sums(j + 1)

@@ -24,6 +24,7 @@ PASS_WORDS = K_PASS // PAIR
 B_TILES = BATCH // P
 CHUNK = 512
 SLABS = HID // CHUNK
+BIAS_ROWS = CELLS * 2 * SLABS
 ROWS = CHUNK // P
 RESULT_BUFS = 20
 
@@ -52,25 +53,27 @@ def tile_compute_gate_e_kernel(tc, input_word, hidden_states, Wx_words, Wx_scale
         wx_planes = keep.tile([P, 2 * HID], U8, name="wx_planes", align_bytes=64)
         nc.vector.memset(wx_planes[:].bitcast(I32), 0)
         bias_rows = keep.tile([P, CHUNK], BF16, name="bias_rows")
-        nc.vector.memset(bias_rows[:], 0.0)
+        nc.sync.dma_start(
+            out=bias_rows[:],
+            in_=bx.rearrange("c (s n) -> (c s) n", n=CHUNK)
+            .unsqueeze(0)
+            .to_broadcast([P // BIAS_ROWS, BIAS_ROWS, CHUNK]),
+        )
+        ident_bf16 = keep.tile([P, P], BF16, name="ident_bf16")
+        make_identity(nc, ident_bf16[:])
+        ident_f32 = keep.tile([P, P], F32, name="ident_f32")
+        make_identity(nc, ident_f32[:])
         warm = keep.tile([P, 1], F32, name="warm")
         nc.vector.memset(warm[:], 0.0)
         nc.scalar.activation(out=warm[:], in_=warm[:], func=ACT.Sigmoid)
-        ident_f32 = keep.tile([P, P], F32, name="ident_f32")
-        make_identity(nc, ident_f32[:])
-        ident_bf16 = keep.tile([P, P], BF16, name="ident_bf16")
-        make_identity(nc, ident_bf16[:])
 
         def load_activations(rows, name):
-            halves = []
-            for half in range(B_TILES // 2):
-                raw = keep.tile([P, 2, K], BF16, name="%s_raw%d" % (name, half))
-                nc.sync.dma_start(
-                    out=raw[:],
-                    in_=rows[2 * P * half : 2 * P * (half + 1), :].rearrange("(t p) k -> p t k", p=P),
-                )
-                halves.append(raw)
-            return halves
+            tiles = []
+            for bt in range(B_TILES):
+                raw = keep.tile([P, K], BF16, name="%s_raw%d" % (name, bt))
+                nc.sync.dma_start(out=raw[:], in_=rows[P * bt : P * (bt + 1), :])
+                tiles.append(raw)
+            return tiles
 
         def load_wx(j):
             cell, n0 = chunks[j][2], chunks[j][4]
@@ -97,7 +100,6 @@ def tile_compute_gate_e_kernel(tc, input_word, hidden_states, Wx_words, Wx_scale
                 out=wx_planes[32 * quadrant : 32 * quadrant + 16, :].bitcast(I32),
                 in_=Wx_scales[:, 4 * quadrant : 4 * quadrant + 4, :].bitcast(I32),
             )
-        nc.sync.dma_start(out=bias_rows[0 : CELLS * 2 * SLABS, :], in_=bx.rearrange("c (s n) -> (c s) n", n=CHUNK))
         wx_words = [load_wx(0)]
         h_raw = load_activations(hidden_states, "h")
         wh_raw = [load_wh(0)]
@@ -105,15 +107,14 @@ def tile_compute_gate_e_kernel(tc, input_word, hidden_states, Wx_words, Wx_scale
             wh_raw.append(load_wh(j))
             wx_words.append(load_wx(j))
 
-        def quantise_activations(raw_halves, word_columns, name):
+        def quantise_activations(words_of, name):
             codes = keep.tile([P, B_TILES, PASSES * P], U32, name="%s_codes" % name, align_bytes=64)
             planes = keep.tile([P, B_TILES, PASSES * P], U8, name="%s_planes" % name, align_bytes=64)
             for bt in range(B_TILES):
-                words = raw_halves[bt // 2][:, bt % 2, :].bitcast(F32)
                 flipped = flip_banks.tile([P, PASSES, PAIR, P], F32, name="flipped", tag="bank")
                 for g in range(PASSES):
                     for u in range(PAIR):
-                        nc.tensor.transpose(flipped[:, g, u, :], words[:, word_columns(g, u)], ident_f32[:])
+                        nc.tensor.transpose(flipped[:, g, u, :], words_of(bt, g, u), ident_f32[:])
                 grouped = act_stage.tile([P, PASSES, P, PACK], BF16, name="grouped", align_bytes=64)
                 copy = nc.scalar.copy if bt % 2 == 0 else nc.vector.tensor_copy
                 copy(out=grouped[:].bitcast(F32), in_=flipped[:].rearrange("p g u b -> p g b u"))
@@ -124,7 +125,7 @@ def tile_compute_gate_e_kernel(tc, input_word, hidden_states, Wx_words, Wx_scale
                 )
             return codes, planes
 
-        bias_all = keep.tile([P, CELLS * 2 * SLABS, CHUNK], BF16, name="bias_all")
+        bias_all = keep.tile([P, BIAS_ROWS, CHUNK], BF16, name="bias_all")
 
         def spread_bias(first_row):
             spread = flip_banks.tile([P, PAIR, CHUNK], BF16, name="spread", tag="bank")
@@ -212,18 +213,21 @@ def tile_compute_gate_e_kernel(tc, input_word, hidden_states, Wx_words, Wx_scale
                 nc.scalar.activation(out=result[:], in_=result[:], func=func)
                 nc.sync.dma_start(out=out[P * bt : P * (bt + 1), cell, out_col : out_col + CHUNK], in_=result[:])
 
-        x_codes, x_planes = quantise_activations(
-            x_raw, lambda g, u: slice(PASS_WORDS * g + u, PASS_WORDS * (g + 1), PAIR), "x"
-        )
-        for cell in range(CELLS):
-            spread_bias(2 * SLABS * cell)
-        sums = open_sums(0)
+        for first_row in range(0, BIAS_ROWS, PAIR):
+            spread_bias(first_row)
+        x_sorted = []
+        for bt in range(B_TILES):
+            by_half = keep.tile([P, PASSES, PAIR, P], F32, name="x_sorted%d" % bt)
+            nc.scalar.copy(
+                out=by_half[:], in_=x_raw[bt][:].bitcast(F32).rearrange("p (g w u) -> p g u w", g=PASSES, u=PAIR)
+            )
+            x_sorted.append(by_half)
+        x_codes, x_planes = quantise_activations(lambda bt, g, u: x_sorted[bt][:, g, u, :], "x")
         h_codes, h_planes = quantise_activations(
-            h_raw, lambda g, u: slice(PASS_WORDS * g + P * u, PASS_WORDS * g + P * (u + 1)), "h"
+            lambda bt, g, u: h_raw[bt][:].bitcast(F32)[:, PASS_WORDS * g + P * u : PASS_WORDS * g + P * (u + 1)], "h"
         )
+        sums = open_sums(0)
         codes, planes = quantise_wh(transpose_wh(0))
-        for cell in range(CELLS):
-            spread_bias(2 * SLABS * cell + SLABS)
         for j in range(n_chunks):
             last = j == n_chunks - 1
             if not last:

@@ -24,7 +24,6 @@ PASS_WORDS = K_PASS // PAIR
 B_TILES = BATCH // P
 CHUNK = 512
 SLABS = HID // CHUNK
-BIAS_ROWS = CELLS * 2 * SLABS
 ROWS = CHUNK // P
 RESULT_BUFS = 20
 
@@ -53,27 +52,25 @@ def tile_compute_gate_e_kernel(tc, input_word, hidden_states, Wx_words, Wx_scale
         wx_planes = keep.tile([P, 2 * HID], U8, name="wx_planes", align_bytes=64)
         nc.vector.memset(wx_planes[:].bitcast(I32), 0)
         bias_rows = keep.tile([P, CHUNK], BF16, name="bias_rows")
-        nc.sync.dma_start(
-            out=bias_rows[:],
-            in_=bx.rearrange("c (s n) -> (c s) n", n=CHUNK)
-            .unsqueeze(0)
-            .to_broadcast([P // BIAS_ROWS, BIAS_ROWS, CHUNK]),
-        )
-        ident_bf16 = keep.tile([P, P], BF16, name="ident_bf16")
-        make_identity(nc, ident_bf16[:])
-        ident_f32 = keep.tile([P, P], F32, name="ident_f32")
-        make_identity(nc, ident_f32[:])
+        nc.vector.memset(bias_rows[:], 0.0)
         warm = keep.tile([P, 1], F32, name="warm")
         nc.vector.memset(warm[:], 0.0)
         nc.scalar.activation(out=warm[:], in_=warm[:], func=ACT.Sigmoid)
+        ident_f32 = keep.tile([P, P], F32, name="ident_f32")
+        make_identity(nc, ident_f32[:])
+        ident_bf16 = keep.tile([P, P], BF16, name="ident_bf16")
+        make_identity(nc, ident_bf16[:])
 
         def load_activations(rows, name):
-            tiles = []
-            for bt in range(B_TILES):
-                raw = keep.tile([P, K], BF16, name="%s_raw%d" % (name, bt))
-                nc.sync.dma_start(out=raw[:], in_=rows[P * bt : P * (bt + 1), :])
-                tiles.append(raw)
-            return tiles
+            halves = []
+            for half in range(B_TILES // 2):
+                raw = keep.tile([P, 2, K], BF16, name="%s_raw%d" % (name, half))
+                nc.sync.dma_start(
+                    out=raw[:],
+                    in_=rows[2 * P * half : 2 * P * (half + 1), :].rearrange("(t p) k -> p t k", p=P),
+                )
+                halves.append(raw)
+            return halves
 
         def load_wx(j):
             cell, n0 = chunks[j][2], chunks[j][4]
@@ -100,21 +97,24 @@ def tile_compute_gate_e_kernel(tc, input_word, hidden_states, Wx_words, Wx_scale
                 out=wx_planes[32 * quadrant : 32 * quadrant + 16, :].bitcast(I32),
                 in_=Wx_scales[:, 4 * quadrant : 4 * quadrant + 4, :].bitcast(I32),
             )
+        nc.sync.dma_start(out=bias_rows[0 : CELLS * 2 * SLABS, :], in_=bx.rearrange("c (s n) -> (c s) n", n=CHUNK))
         wx_words = [load_wx(0)]
         h_raw = load_activations(hidden_states, "h")
-        wh_raw = [load_wh(0)]
+        wh_raw = [load_wh(0), load_wh(1)]
         for j in range(1, n_chunks):
-            wh_raw.append(load_wh(j))
+            if j + 1 < n_chunks:
+                wh_raw.append(load_wh(j + 1))
             wx_words.append(load_wx(j))
 
-        def quantise_activations(words_of, name):
+        def quantise_activations(raw_halves, word_columns, name):
             codes = keep.tile([P, B_TILES, PASSES * P], U32, name="%s_codes" % name, align_bytes=64)
             planes = keep.tile([P, B_TILES, PASSES * P], U8, name="%s_planes" % name, align_bytes=64)
             for bt in range(B_TILES):
+                words = raw_halves[bt // 2][:, bt % 2, :].bitcast(F32)
                 flipped = flip_banks.tile([P, PASSES, PAIR, P], F32, name="flipped", tag="bank")
                 for g in range(PASSES):
                     for u in range(PAIR):
-                        nc.tensor.transpose(flipped[:, g, u, :], words_of(bt, g, u), ident_f32[:])
+                        nc.tensor.transpose(flipped[:, g, u, :], words[:, word_columns(g, u)], ident_f32[:])
                 grouped = act_stage.tile([P, PASSES, P, PACK], BF16, name="grouped", align_bytes=64)
                 copy = nc.scalar.copy if bt % 2 == 0 else nc.vector.tensor_copy
                 copy(out=grouped[:].bitcast(F32), in_=flipped[:].rearrange("p g u b -> p g b u"))
@@ -125,7 +125,7 @@ def tile_compute_gate_e_kernel(tc, input_word, hidden_states, Wx_words, Wx_scale
                 )
             return codes, planes
 
-        bias_all = keep.tile([P, BIAS_ROWS, CHUNK], BF16, name="bias_all")
+        bias_all = keep.tile([P, CELLS * 2 * SLABS, CHUNK], BF16, name="bias_all")
 
         def spread_bias(first_row):
             spread = flip_banks.tile([P, PAIR, CHUNK], BF16, name="spread", tag="bank")
@@ -213,26 +213,24 @@ def tile_compute_gate_e_kernel(tc, input_word, hidden_states, Wx_words, Wx_scale
                 nc.scalar.activation(out=result[:], in_=result[:], func=func)
                 nc.sync.dma_start(out=out[P * bt : P * (bt + 1), cell, out_col : out_col + CHUNK], in_=result[:])
 
-        for first_row in range(0, BIAS_ROWS, PAIR):
-            spread_bias(first_row)
-        x_sorted = []
-        for bt in range(B_TILES):
-            by_half = keep.tile([P, PASSES, PAIR, P], F32, name="x_sorted%d" % bt)
-            nc.scalar.copy(
-                out=by_half[:], in_=x_raw[bt][:].bitcast(F32).rearrange("p (g w u) -> p g u w", g=PASSES, u=PAIR)
-            )
-            x_sorted.append(by_half)
-        x_codes, x_planes = quantise_activations(lambda bt, g, u: x_sorted[bt][:, g, u, :], "x")
-        h_codes, h_planes = quantise_activations(
-            lambda bt, g, u: h_raw[bt][:].bitcast(F32)[:, PASS_WORDS * g + P * u : PASS_WORDS * g + P * (u + 1)], "h"
+        x_codes, x_planes = quantise_activations(
+            x_raw, lambda g, u: slice(PASS_WORDS * g + u, PASS_WORDS * (g + 1), PAIR), "x"
         )
+        for cell in range(CELLS):
+            spread_bias(2 * SLABS * cell)
         sums = open_sums(0)
+        h_codes, h_planes = quantise_activations(
+            h_raw, lambda g, u: slice(PASS_WORDS * g + P * u, PASS_WORDS * g + P * (u + 1)), "h"
+        )
         codes, planes = quantise_wh(transpose_wh(0))
+        for cell in range(CELLS):
+            spread_bias(2 * SLABS * cell + SLABS)
+        wh_grouped = {1: transpose_wh(1)}
         for j in range(n_chunks):
-            last = j == n_chunks - 1
-            if not last:
-                next_grouped = transpose_wh(j + 1)
             close_sums(j, sums, codes, planes)
-            if not last:
-                codes, planes = quantise_wh(next_grouped)
+            if j + 1 < n_chunks:
+                codes, planes = quantise_wh(wh_grouped[j + 1])
+            if j + 2 < n_chunks:
+                wh_grouped[j + 2] = transpose_wh(j + 2)
+            if j + 1 < n_chunks:
                 sums = open_sums(j + 1)

from contextlib import ExitStack

import concourse.mybir as mybir
from concourse.masks import make_identity

F32 = mybir.dt.float32
BF16 = mybir.dt.bfloat16
I32 = mybir.dt.int32
U32 = mybir.dt.uint32
U8 = mybir.dt.uint8
FP8X4 = mybir.dt.float8_e4m3fn_x4
ACT = mybir.ActivationFunctionType

P = 128
PACK = 4
PAIR = 2
K_PASS = P * PACK
BATCH = 512
K = 1024
HID = 1024
CELLS = 2
PASSES = K // K_PASS
PASS_WORDS = K_PASS // PAIR
B_TILES = BATCH // P
CHUNK = 512
SLABS = HID // CHUNK
ROWS = CHUNK // P
RESULT_BUFS = 20

FLOPS = 2 * BATCH * (CELLS * 2 * HID) * (2 * K)


def tile_compute_gate_e_kernel(tc, input_word, hidden_states, Wx_words, Wx_scales, bx, Wh, out_0, out_1):
    nc = tc.nc

    chunks = []
    for func, out, first_n in ((ACT.Sigmoid, out_1, 0), (ACT.Tanh, out_0, HID)):
        for cell in range(CELLS):
            for slab in range(SLABS):
                chunks.append((func, out, cell, slab * CHUNK, first_n + slab * CHUNK))
    n_chunks = len(chunks)

    with ExitStack() as ctx:
        keep = ctx.enter_context(tc.tile_pool(name="keep", bufs=1))
        act_stage = ctx.enter_context(tc.tile_pool(name="act_stage", bufs=3))
        wh_stage = ctx.enter_context(tc.tile_pool(name="wh_stage", bufs=2))
        results = ctx.enter_context(tc.tile_pool(name="results", bufs=RESULT_BUFS))
        flip_banks = ctx.enter_context(tc.psum_pool(name="flip_banks", bufs=4))
        sum_banks = ctx.enter_context(tc.psum_pool(name="sum_banks", bufs=B_TILES))
        ctx.enter_context(tc.manual_schedule())

        wx_planes = keep.tile([P, 2 * HID], U8, name="wx_planes", align_bytes=64)
        nc.vector.memset(wx_planes[:].bitcast(I32), 0)
        bias_rows = keep.tile([P, CHUNK], BF16, name="bias_rows")
        nc.vector.memset(bias_rows[:], 0.0)
        warm = keep.tile([P, 1], F32, name="warm")
        nc.vector.memset(warm[:], 0.0)
        nc.scalar.activation(out=warm[:], in_=warm[:], func=ACT.Sigmoid)
        ident_f32 = keep.tile([P, P], F32, name="ident_f32")
        make_identity(nc, ident_f32[:])
        ident_bf16 = keep.tile([P, P], BF16, name="ident_bf16")
        make_identity(nc, ident_bf16[:])

        def load_activations(rows, name):
            halves = []
            for half in range(B_TILES // 2):
                raw = keep.tile([P, 2, K], BF16, name="%s_raw%d" % (name, half))
                nc.sync.dma_start(
                    out=raw[:],
                    in_=rows[2 * P * half : 2 * P * (half + 1), :].rearrange("(t p) k -> p t k", p=P),
                )
                halves.append(raw)
            return halves

        def load_wx(j):
            cell, n0 = chunks[j][2], chunks[j][4]
            words = keep.tile([P, PASSES, CHUNK], U32, name="wx_words%d" % j, align_bytes=64)
            nc.sync.dma_start(
                out=words[:].bitcast(I32),
                in_=Wx_words[PASSES * cell : PASSES * (cell + 1), :, n0 : n0 + CHUNK, :]
                .rearrange("g p n t -> p g (n t)")
                .bitcast(I32),
            )
            return words

        def load_wh(j):
            cell, n0 = chunks[j][2], chunks[j][4]
            raw = keep.tile([P, ROWS, K], BF16, name="wh_raw%d" % j)
            rows = Wh[cell, n0 : n0 + CHUNK, :].rearrange("(q r) k -> q r k", r=ROWS)
            for first in range(0, ROWS, PAIR):
                nc.sync.dma_start(out=raw[:, first : first + PAIR, :], in_=rows[:, first : first + PAIR, :])
            return raw

        x_raw = load_activations(input_word, "x")
        for quadrant in range(4):
            nc.sync.dma_start(
                out=wx_planes[32 * quadrant : 32 * quadrant + 16, :].bitcast(I32),
                in_=Wx_scales[:, 4 * quadrant : 4 * quadrant + 4, :].bitcast(I32),
            )
        nc.sync.dma_start(out=bias_rows[0 : CELLS * 2 * SLABS, :], in_=bx.rearrange("c (s n) -> (c s) n", n=CHUNK))
        wx_words = [load_wx(0)]
        h_raw = load_activations(hidden_states, "h")
        wh_raw = [load_wh(0), load_wh(1)]
        for j in range(1, n_chunks):
            if j + 1 < n_chunks:
                wh_raw.append(load_wh(j + 1))
            wx_words.append(load_wx(j))

        def quantise_activations(raw_halves, word_columns, name):
            codes = keep.tile([P, B_TILES, PASSES * P], U32, name="%s_codes" % name, align_bytes=64)
            planes = keep.tile([P, B_TILES, PASSES * P], U8, name="%s_planes" % name, align_bytes=64)
            for bt in range(B_TILES):
                words = raw_halves[bt // 2][:, bt % 2, :].bitcast(F32)
                flipped = flip_banks.tile([P, PASSES, PAIR, P], F32, name="flipped", tag="bank")
                for g in range(PASSES):
                    for u in range(PAIR):
                        nc.tensor.transpose(flipped[:, g, u, :], words[:, word_columns(g, u)], ident_f32[:])
                grouped = act_stage.tile([P, PASSES, P, PACK], BF16, name="grouped", align_bytes=64)
                copy = nc.scalar.copy if bt % 2 == 0 else nc.vector.tensor_copy
                copy(out=grouped[:].bitcast(F32), in_=flipped[:].rearrange("p g u b -> p g b u"))
                nc.vector.quantize_mx(
                    out=codes[:, bt, :].bitcast(FP8X4),
                    scales=planes[:, bt, :],
                    in_=grouped[:].rearrange("p g b t -> p (g b t)"),
                )
            return codes, planes

        bias_all = keep.tile([P, CELLS * 2 * SLABS, CHUNK], BF16, name="bias_all")

        def spread_bias(first_row):
            spread = flip_banks.tile([P, PAIR, CHUNK], BF16, name="spread", tag="bank")
            for i in range(PAIR):
                row = first_row + i
                nc.tensor.matmul(
                    spread[:, i, :],
                    lhsT=ident_bf16[:, row : row + 1].to_broadcast([P, P]),
                    rhs=bias_rows[:],
                    start=True,
                    stop=True,
                )
            nc.vector.tensor_copy(out=bias_all[:, first_row : first_row + PAIR, :], in_=spread[:])

        def transpose_wh(j):
            words = wh_raw[j][:].bitcast(F32)
            grouped = wh_stage.tile([P, PASSES, CHUNK, PACK], BF16, name="wh_grouped", align_bytes=64)
            for first in range(0, ROWS, PAIR):
                for g in range(PASSES):
                    flipped = flip_banks.tile([P, PAIR, PAIR, P], F32, name="flipped", tag="bank")
                    for r in range(PAIR):
                        for u in range(PAIR):
                            start_word = PASS_WORDS * g + P * u
                            nc.tensor.transpose(
                                flipped[:, r, u, :], words[:, first + r, start_word : start_word + P], ident_f32[:]
                            )
                    nc.scalar.copy(
                        out=grouped[:, g].bitcast(F32).rearrange("p (q r) u -> p q r u", r=ROWS)[
                            :, :, first : first + PAIR, :
                        ],
                        in_=flipped[:].rearrange("p r u q -> p q r u"),
                    )
            return grouped

        def quantise_wh(grouped):
            codes = wh_stage.tile([P, PASSES, CHUNK], U32, name="wh_codes", align_bytes=64)
            planes = wh_stage.tile([P, PASSES, CHUNK], U8, name="wh_planes", align_bytes=64)
            for g in range(PASSES):
                nc.vector.quantize_mx(
                    out=codes[:, g, :].bitcast(FP8X4),
                    scales=planes[:, g, :],
                    in_=grouped[:, g].rearrange("p n t -> p (n t)"),
                )
            return codes, planes

        def open_sums(j):
            cell, n0 = chunks[j][2], chunks[j][4]
            sums = []
            for bt in range(B_TILES):
                bank = sum_banks.tile([P, CHUNK], F32, name="sums")
                for g in range(PASSES):
                    nc.tensor.matmul_mx(
                        out=bank[:],
                        lhsT=x_codes[:, bt, P * g : P * (g + 1)].bitcast(FP8X4),
                        lhsT_scale=x_planes[:, bt, P * g : P * (g + 1)],
                        rhs=wx_words[j][:, g, :].bitcast(FP8X4),
                        rhs_scale=wx_planes[4 * (PASSES * cell + g) : P, n0 : n0 + CHUNK],
                        start=(g == 0),
                        stop=False,
                    )
                sums.append(bank)
            return sums

        def close_sums(j, sums, codes, planes):
            func, out, cell, out_col, n0 = chunks[j]
            for bt in range(B_TILES):
                for g in range(PASSES):
                    nc.tensor.matmul_mx(
                        out=sums[bt][:],
                        lhsT=h_codes[:, bt, P * g : P * (g + 1)].bitcast(FP8X4),
                        lhsT_scale=h_planes[:, bt, P * g : P * (g + 1)],
                        rhs=codes[:, g, :].bitcast(FP8X4),
                        rhs_scale=planes[:, g, :],
                        start=False,
                        stop=(g == PASSES - 1),
                    )
            for bt in range(B_TILES):
                result = results.tile([P, CHUNK], F32, name="result")
                nc.vector.tensor_tensor(
                    out=result[:],
                    in0=sums[bt][:],
                    in1=bias_all[:, 2 * SLABS * cell + n0 // CHUNK, :],
                    op=mybir.AluOpType.add,
                )
                nc.scalar.activation(out=result[:], in_=result[:], func=func)
                nc.sync.dma_start(out=out[P * bt : P * (bt + 1), cell, out_col : out_col + CHUNK], in_=result[:])

        x_codes, x_planes = quantise_activations(
            x_raw, lambda g, u: slice(PASS_WORDS * g + u, PASS_WORDS * (g + 1), PAIR), "x"
        )
        for cell in range(CELLS):
            spread_bias(2 * SLABS * cell)
        sums = open_sums(0)
        h_codes, h_planes = quantise_activations(
            h_raw, lambda g, u: slice(PASS_WORDS * g + P * u, PASS_WORDS * g + P * (u + 1)), "h"
        )
        codes, planes = quantise_wh(transpose_wh(0))
        for cell in range(CELLS):
            spread_bias(2 * SLABS * cell + SLABS)
        wh_grouped = {1: transpose_wh(1)}
        for j in range(n_chunks):
            close_sums(j, sums, codes, planes)
            if j + 1 < n_chunks:
                codes, planes = quantise_wh(wh_grouped[j + 1])
            if j + 2 < n_chunks:
                wh_grouped[j + 2] = transpose_wh(j + 2)
            if j + 1 < n_chunks:
                sums = open_sums(j + 1)
